import numpy as np
import ml_dtypes


def mxq(x, axis, fmt="e4m3"):
    dtype, down = {"e4m3": (ml_dtypes.float8_e4m3fn, 7), "e5m2": (ml_dtypes.float8_e5m2, 14)}[fmt]
    v = np.moveaxis(np.asarray(x, np.float32).astype(ml_dtypes.bfloat16).astype(np.float64), axis, -1)
    blocks = v.reshape(v.shape[:-1] + (-1, 32))
    amax = np.abs(blocks).max(-1, keepdims=True)
    byte = np.maximum(np.where(amax > 0, np.frexp(amax)[1] - 1 + 127, 0) - down, 1)
    scale = np.exp2(byte - 127.0)
    codes = (blocks / scale).astype(np.float32).astype(dtype).astype(np.float64)
    return np.moveaxis((codes * scale).reshape(v.shape), -1, axis)


WIDE = False


def mx_kscale(k):
    if not WIDE:
        return np.ones(k)
    levels = np.array([10, -10, 5, -5, 0])
    a = np.random.permutation(np.resize(levels, k // 512 * 4)).reshape(k // 512, 4)
    idx = np.arange(k)
    return np.exp2(a[idx // 512, idx % 128 // 32])


BF16 = ml_dtypes.bfloat16


def bf(x):
    return np.asarray(x, np.float32).astype(BF16)


def f64(x):
    return np.asarray(x).astype(np.float64)


B, T, D, N, M = 2, 64, 512, 1024, 512
EPS = 1e-12


def softmax(v):
    e = np.exp(v - v.max(-1, keepdims=True))
    return e / e.sum(-1, keepdims=True)


def l2n(v):
    return v * (1.0 / np.sqrt(np.maximum((v * v).sum(-1, keepdims=True), EPS)))


def setup_inputs():
    s = mx_kscale(D)
    return {"controller_output": bf(np.random.standard_normal((B, T, D)) * s),
            "Wk": bf(np.random.standard_normal((D, M)) / np.sqrt(D) / s[:, None]),
            "bk": bf(np.random.standard_normal(M) * 0.5),
            "memory": bf(np.random.standard_normal((N, M)) * 0.5 / N)}


def reference(controller_output, Wk, bk, memory):
    z = (mxq(f64(controller_output), 2, "e4m3") @ mxq(f64(Wk), 0, "e4m3")) + f64(bk)
    kn = l2n(softmax(z))
    mn = l2n(f64(memory))
    sims = -(mxq(kn, 2, "e4m3") @ mxq(mn, 1, "e4m3").T)
    return softmax(sims)

@@ -1,0 +1,247 @@
+from contextlib import ExitStack
+
+import concourse.mybir as mybir
+from concourse.masks import make_identity
+
+F32 = mybir.dt.float32
+BF16 = mybir.dt.bfloat16
+U32 = mybir.dt.uint32
+U8 = mybir.dt.uint8
+FP8X4 = mybir.dt.float8_e4m3fn_x4
+ALU = mybir.AluOpType
+ACT = mybir.ActivationFunctionType
+AXIS_X = mybir.AxisListType.X
+
+P = 128
+K = 512
+PACK = 4
+HALVES = 2
+SLOTS = 1024
+SLOT_TILES = SLOTS // P
+PAIRS = SLOT_TILES // 2
+BANK = 512
+NORM_FLOOR = 1e-12
+
+FLOPS = 2 * P * K * K + 2 * P * K * SLOTS
+
+
+def transpose_words(nc, identity, planes, rows):
+    words = rows.bitcast(F32)
+    for u in range(HALVES):
+        nc.tensor.transpose(planes[:, u, :], words[:, u * P : (u + 1) * P], identity)
+
+
+def quantise(nc, codes, scales, grouped):
+    nc.vector.quantize_mx(out=codes.bitcast(FP8X4), scales=scales, in_=grouped)
+
+
+def tile_contentaddressablewritehead_pa_s_kernel(tc, controller_output, Wk, bk, memory, out):
+    nc = tc.nc
+    with ExitStack() as ctx:
+        const = ctx.enter_context(tc.tile_pool(name="const", bufs=1))
+        keep = ctx.enter_context(tc.tile_pool(name="keep", bufs=1))
+        pairs = ctx.enter_context(tc.tile_pool(name="pairs", bufs=PAIRS))
+        psum_words = ctx.enter_context(tc.psum_pool(name="psum_words", bufs=4))
+        psum_sums = ctx.enter_context(tc.psum_pool(name="psum_sums", bufs=1))
+        ctx.enter_context(tc.manual_schedule())
+
+        memory_tiles = memory.rearrange("(j p) k -> p j k", p=P)
+        memory_pairs = []
+        for g in range(PAIRS):
+            memory_pair = pairs.tile([P, 2, K], BF16)
+            memory_pairs.append(memory_pair)
+        wk_rows = keep.tile([P, PACK, K], BF16)
+        x_rows = keep.tile([P, K], BF16)
+        bias_rows = const.tile([P, K], BF16)
+        nc.vector.memset(bias_rows[:], 0.0)
+        nc.scalar.dma_start(out=bias_rows[0:1, :], in_=bk.rearrange("(o m) -> o m", o=1))
+        nc.sync.dma_start(out=memory_pairs[0][:], in_=memory_tiles[:, 0:2, :])
+        nc.sync.dma_start(
+            out=wk_rows[:].rearrange("p (u e) c -> p u (e c)", u=HALVES),
+            in_=Wk.rearrange("(u p e) c -> p u (e c)", u=HALVES, e=2),
+        )
+        nc.sync.dma_start(out=x_rows[:], in_=controller_output.flatten_outer_dims())
+        for g in range(1, PAIRS):
+            nc.sync.dma_start(out=memory_pairs[g][:], in_=memory_tiles[:, 2 * g : 2 * g + 2, :])
+
+        minus_half = const.tile([P, 2], F32)
+        nc.gpsimd.memset(minus_half[:], -0.5)
+        identity = const.tile([P, P], F32)
+        make_identity(nc, identity[:])
+        ones = const.tile([P, P], BF16)
+        nc.vector.memset(ones[:], 1.0)
+        table_warmer = const.tile([P, 1], F32)
+        nc.scalar.activation(out=table_warmer[:], in_=minus_half[:, 0:1], func=ACT.Exp)
+
+        mn_codes = keep.tile([P, SLOTS], U32, align_bytes=64)
+        mn_scales = keep.tile([P, SLOTS], U8, align_bytes=64)
+        inverse_lengths = []
+        planes_of_pair = []
+
+        def measure(g):
+            squares = pairs.tile([P, 2, K], BF16)
+            sum_squares = pairs.tile([P, 2], F32)
+            for i in range(2):
+                nc.scalar.activation(
+                    out=squares[:, i, :],
+                    in_=memory_pairs[g][:, i, :],
+                    func=ACT.Square,
+                    accum_out=sum_squares[:, i : i + 1],
+                )
+            floored = pairs.tile([P, 2], F32)
+            nc.gpsimd.tensor_scalar_max(out=floored[:], in0=sum_squares[:], scalar1=NORM_FLOOR)
+            inverse_length = pairs.tile([P, 2], F32)
+            nc.gpsimd.tensor_tensor(out=inverse_length[:], in0=floored[:], in1=minus_half[:], op=ALU.pow)
+            inverse_lengths.append(inverse_length)
+
+        def normalise_and_transpose(g):
+            mn_rows = pairs.tile([P, 2, K], BF16)
+            mn_planes = psum_words.tile([P, 2, HALVES, P], F32, tag="planes")
+            for i in range(2):
+                nc.vector.tensor_scalar(
+                    out=mn_rows[:, i, :],
+                    in0=memory_pairs[g][:, i, :],
+                    scalar1=inverse_lengths[g][:, i : i + 1],
+                    scalar2=None,
+                    op0=ALU.mult,
+                )
+                transpose_words(nc, identity[:], mn_planes[:, i, :, :], mn_rows[:, i, :])
+            planes_of_pair.append(mn_planes)
+
+        grouped_of_pair = []
+
+        def interleave(g, copy):
+            mn_grouped = pairs.tile([P, 2 * P * PACK], BF16, align_bytes=64)
+            copy(
+                out=mn_grouped[:].bitcast(F32).rearrange("p (i r u) -> p i r u", i=2, u=HALVES),
+                in_=planes_of_pair[g][:].rearrange("p i u r -> p i r u"),
+            )
+            grouped_of_pair.append(mn_grouped)
+
+        def quantise_pair(g):
+            pair_slots = slice(2 * P * g, 2 * P * (g + 1))
+            quantise(nc, mn_codes[:, pair_slots], mn_scales[:, pair_slots], grouped_of_pair[g][:])
+
+        measure(0)
+
+        wk_grouped = keep.tile([P, K, PACK], BF16, align_bytes=64)
+        nc.vector.tensor_copy(
+            out=wk_grouped[:].rearrange("p (c i) t -> p c t i", i=4),
+            in_=wk_rows[:].rearrange("p t (c i) -> p c t i", i=4),
+        )
+
+        x_planes = psum_words.tile([P, HALVES, P], F32, tag="planes")
+        transpose_words(nc, identity[:], x_planes, x_rows[:])
+        x_grouped = keep.tile([P, P * PACK], BF16, align_bytes=64)
+        nc.scalar.copy(
+            out=x_grouped[:].bitcast(F32).rearrange("p (r u) -> p r u", u=HALVES),
+            in_=x_planes[:].rearrange("p u r -> p r u"),
+        )
+        bias_sum = psum_sums.tile([P, K], F32)
+        nc.tensor.matmul(out=bias_sum[:], lhsT=ones[:], rhs=bias_rows[:], start=True, stop=True)
+        bias = const.tile([P, K], F32)
+        nc.scalar.copy(out=bias[:], in_=bias_sum[:])
+
+        x_codes = keep.tile([P, P], U32, align_bytes=64)
+        x_scales = keep.tile([P, P], U8, align_bytes=64)
+        quantise(nc, x_codes[:], x_scales[:], x_grouped[:])
+        wk_codes = keep.tile([P, K], U32, align_bytes=64)
+        wk_scales = keep.tile([P, K], U8, align_bytes=64)
+        quantise(nc, wk_codes[:], wk_scales[:], wk_grouped[:].rearrange("p c t -> p (c t)"))
+
+        z_sum = psum_sums.tile([P, K], F32)
+        nc.tensor.matmul_mx(
+            out=z_sum[:],
+            lhsT=x_codes[:].bitcast(FP8X4),
+            lhsT_scale=x_scales[:],
+            rhs=wk_codes[:].bitcast(FP8X4),
+            rhs_scale=wk_scales[:],
+            start=True,
+            stop=True,
+        )
+        for g in range(1, PAIRS):
+            measure(g)
+        normalise_and_transpose(0)
+        z = keep.tile([P, K], F32)
+        nc.vector.tensor_tensor(out=z[:], in0=z_sum[:], in1=bias[:], op=ALU.add)
+        interleave(0, nc.vector.tensor_copy)
+
+        minus_max = keep.tile([P, 1], F32)
+        nc.vector.tensor_reduce(out=minus_max[:], in_=z[:], axis=AXIS_X, op=ALU.max, negate=True)
+        quantise_pair(0)
+        minus_2max = keep.tile([P, 1], F32)
+        nc.vector.tensor_scalar_mul(out=minus_2max[:], in0=minus_max[:], scalar1=2.0)
+        e_squared = keep.tile([P, K], BF16)
+        e_sum_squares = keep.tile([P, 1], F32)
+        nc.scalar.activation(
+            out=e_squared[:], in_=z[:], func=ACT.Exp, bias=minus_2max[:], scale=2.0, accum_out=e_sum_squares[:]
+        )
+        e = keep.tile([P, K], F32)
+        nc.scalar.activation(out=e[:], in_=z[:], func=ACT.Exp, bias=minus_max[:], scale=1.0)
+        e_inverse_length = keep.tile([P, 1], F32)
+        nc.gpsimd.tensor_tensor(
+            out=e_inverse_length[:], in0=e_sum_squares[:], in1=minus_half[:, 0:1], op=ALU.pow
+        )
+        for g in range(1, PAIRS):
+            normalise_and_transpose(g)
+        interleave(1, nc.vector.tensor_copy)
+        interleave(2, nc.scalar.copy)
+        interleave(3, nc.scalar.copy)
+        kn_rows = keep.tile([P, K], BF16)
+        nc.vector.tensor_scalar(
+            out=kn_rows[:], in0=e[:], scalar1=e_inverse_length[:, 0:1], scalar2=None, op0=ALU.mult
+        )
+        kn_planes = psum_words.tile([P, HALVES, P], F32, tag="planes")
+        transpose_words(nc, identity[:], kn_planes, kn_rows[:])
+        quantise_pair(1)
+        quantise_pair(2)
+        kn_grouped = keep.tile([P, P * PACK], BF16, align_bytes=64)
+        nc.vector.tensor_copy(
+            out=kn_grouped[:].bitcast(F32).rearrange("p (r u) -> p r u", u=HALVES),
+            in_=kn_planes[:].rearrange("p u r -> p r u"),
+        )
+        quantise_pair(3)
+        kn_codes = keep.tile([P, P], U32, align_bytes=64)
+        kn_scales = keep.tile([P, P], U8, align_bytes=64)
+        quantise(nc, kn_codes[:], kn_scales[:], kn_grouped[:])
+
+        sims = []
+        sims_min_by_bank = keep.tile([P, SLOTS // BANK], F32)
+        for b in range(SLOTS // BANK):
+            bank_slots = slice(BANK * b, BANK * (b + 1))
+            sims_bank = psum_sums.tile([P, BANK], F32, name="sims%d" % b)
+            nc.tensor.matmul_mx(
+                out=sims_bank[:],
+                lhsT=kn_codes[:].bitcast(FP8X4),
+                lhsT_scale=kn_scales[:],
+                rhs=mn_codes[:, bank_slots].bitcast(FP8X4),
+                rhs_scale=mn_scales[:, bank_slots],
+                start=True,
+                stop=True,
+            )
+            nc.vector.tensor_reduce(out=sims_min_by_bank[:, b : b + 1], in_=sims_bank[:], axis=AXIS_X, op=ALU.min)
+            sims.append(sims_bank)
+        sims_min = keep.tile([P, 1], F32)
+        nc.vector.tensor_reduce(out=sims_min[:], in_=sims_min_by_bank[:], axis=AXIS_X, op=ALU.min)
+        weights = keep.tile([P, SLOTS], F32)
+        sum_by_bank = keep.tile([P, SLOTS // BANK], F32)
+        for b in range(SLOTS // BANK):
+            nc.scalar.activation(
+                out=weights[:, BANK * b : BANK * (b + 1)],
+                in_=sims[b][:],
+                func=ACT.Exp,
+                bias=sims_min[:],
+                scale=-1.0,
+                accum_out=sum_by_bank[:, b : b + 1],
+            )
+        weight_sum = keep.tile([P, 1], F32)
+        nc.vector.tensor_reduce(out=weight_sum[:], in_=sum_by_bank[:], axis=AXIS_X, op=ALU.add)
+        inverse_sum = keep.tile([P, 1], F32)
+        nc.vector.reciprocal(out=inverse_sum[:], in_=weight_sum[:])
+        out_rows = out.flatten_outer_dims()
+        for b in range(SLOTS // BANK):
+            bank_slots = slice(BANK * b, BANK * (b + 1))
+            nc.vector.tensor_scalar(
+                out=weights[:, bank_slots], in0=weights[:, bank_slots], scalar1=inverse_sum[:, 0:1], scalar2=None, op0=ALU.mult
+            )
+            nc.sync.dma_start(out=out_rows[:, bank_slots], in_=weights[:, bank_slots])

@@ -21,6 +21,7 @@ SLOT_TILES = SLOTS // P
 PAIRS = SLOT_TILES // 2
 BANK = 512
 NORM_FLOOR = 1e-12
+WK_VECTOR_COLS = 384
 
 FLOPS = 2 * P * K * K + 2 * P * K * SLOTS
 
@@ -76,7 +77,9 @@ def tile_contentaddressablewritehead_pa_s_kernel(tc, controller_output, Wk, bk, 
         mn_codes = keep.tile([P, SLOTS], U32, align_bytes=64)
         mn_scales = keep.tile([P, SLOTS], U8, align_bytes=64)
         inverse_lengths = []
+        rows_of_pair = []
         planes_of_pair = []
+        grouped_of_pair = []
 
         def measure(g):
             squares = pairs.tile([P, 2, K], BF16)
@@ -94,9 +97,8 @@ def tile_contentaddressablewritehead_pa_s_kernel(tc, controller_output, Wk, bk, 
             nc.gpsimd.tensor_tensor(out=inverse_length[:], in0=floored[:], in1=minus_half[:], op=ALU.pow)
             inverse_lengths.append(inverse_length)
 
-        def normalise_and_transpose(g):
+        def normalise(g):
             mn_rows = pairs.tile([P, 2, K], BF16)
-            mn_planes = psum_words.tile([P, 2, HALVES, P], F32, tag="planes")
             for i in range(2):
                 nc.vector.tensor_scalar(
                     out=mn_rows[:, i, :],
@@ -105,10 +107,13 @@ def tile_contentaddressablewritehead_pa_s_kernel(tc, controller_output, Wk, bk, 
                     scalar2=None,
                     op0=ALU.mult,
                 )
-                transpose_words(nc, identity[:], mn_planes[:, i, :, :], mn_rows[:, i, :])
-            planes_of_pair.append(mn_planes)
+            rows_of_pair.append(mn_rows)
 
-        grouped_of_pair = []
+        def transpose_pair(g):
+            mn_planes = psum_words.tile([P, 2, HALVES, P], F32, tag="planes")
+            for i in range(2):
+                transpose_words(nc, identity[:], mn_planes[:, i, :, :], rows_of_pair[g][:, i, :])
+            planes_of_pair.append(mn_planes)
 
         def interleave(g, copy):
             mn_grouped = pairs.tile([P, 2 * P * PACK], BF16, align_bytes=64)
@@ -126,8 +131,12 @@ def tile_contentaddressablewritehead_pa_s_kernel(tc, controller_output, Wk, bk, 
 
         wk_grouped = keep.tile([P, K, PACK], BF16, align_bytes=64)
         nc.vector.tensor_copy(
-            out=wk_grouped[:].rearrange("p (c i) t -> p c t i", i=4),
-            in_=wk_rows[:].rearrange("p t (c i) -> p c t i", i=4),
+            out=wk_grouped[:, :WK_VECTOR_COLS, :].rearrange("p (c i) t -> p c t i", i=4),
+            in_=wk_rows[:, :, :WK_VECTOR_COLS].rearrange("p t (c i) -> p c t i", i=4),
+        )
+        nc.scalar.copy(
+            out=wk_grouped[:, WK_VECTOR_COLS:, :].rearrange("p (c i) t -> p c t i", i=4),
+            in_=wk_rows[:, :, WK_VECTOR_COLS:].rearrange("p t (c i) -> p c t i", i=4),
         )
 
         x_planes = psum_words.tile([P, HALVES, P], F32, tag="planes")
@@ -137,17 +146,17 @@ def tile_contentaddressablewritehead_pa_s_kernel(tc, controller_output, Wk, bk, 
             out=x_grouped[:].bitcast(F32).rearrange("p (r u) -> p r u", u=HALVES),
             in_=x_planes[:].rearrange("p u r -> p r u"),
         )
-        bias_sum = psum_sums.tile([P, K], F32)
-        nc.tensor.matmul(out=bias_sum[:], lhsT=ones[:], rhs=bias_rows[:], start=True, stop=True)
-        bias = const.tile([P, K], F32)
-        nc.scalar.copy(out=bias[:], in_=bias_sum[:])
-
-        x_codes = keep.tile([P, P], U32, align_bytes=64)
-        x_scales = keep.tile([P, P], U8, align_bytes=64)
-        quantise(nc, x_codes[:], x_scales[:], x_grouped[:])
         wk_codes = keep.tile([P, K], U32, align_bytes=64)
         wk_scales = keep.tile([P, K], U8, align_bytes=64)
         quantise(nc, wk_codes[:], wk_scales[:], wk_grouped[:].rearrange("p c t -> p (c t)"))
+        x_codes = keep.tile([P, P], U32, align_bytes=64)
+        x_scales = keep.tile([P, P], U8, align_bytes=64)
+        quantise(nc, x_codes[:], x_scales[:], x_grouped[:])
+
+        bias_sum = psum_sums.tile([P, K], F32)
+        nc.tensor.matmul(out=bias_sum[:], lhsT=ones[:], rhs=bias_rows[:], start=True, stop=True)
+        bias = const.tile([P, K], F32)
+        nc.vector.tensor_copy(out=bias[:], in_=bias_sum[:])
 
         z_sum = psum_sums.tile([P, K], F32)
         nc.tensor.matmul_mx(
@@ -161,14 +170,14 @@ def tile_contentaddressablewritehead_pa_s_kernel(tc, controller_output, Wk, bk, 
         )
         for g in range(1, PAIRS):
             measure(g)
-        normalise_and_transpose(0)
+        normalise(0)
+        transpose_pair(0)
         z = keep.tile([P, K], F32)
         nc.vector.tensor_tensor(out=z[:], in0=z_sum[:], in1=bias[:], op=ALU.add)
-        interleave(0, nc.vector.tensor_copy)
 
         minus_max = keep.tile([P, 1], F32)
         nc.vector.tensor_reduce(out=minus_max[:], in_=z[:], axis=AXIS_X, op=ALU.max, negate=True)
-        quantise_pair(0)
+        interleave(0, nc.vector.tensor_copy)
         minus_2max = keep.tile([P, 1], F32)
         nc.vector.tensor_scalar_mul(out=minus_2max[:], in0=minus_max[:], scalar1=2.0)
         e_squared = keep.tile([P, K], BF16)
@@ -182,31 +191,34 @@ def tile_contentaddressablewritehead_pa_s_kernel(tc, controller_output, Wk, bk, 
         nc.gpsimd.tensor_tensor(
             out=e_inverse_length[:], in0=e_sum_squares[:], in1=minus_half[:, 0:1], op=ALU.pow
         )
-        for g in range(1, PAIRS):
-            normalise_and_transpose(g)
-        interleave(1, nc.vector.tensor_copy)
-        interleave(2, nc.scalar.copy)
-        interleave(3, nc.scalar.copy)
+        for g in (1, 2):
+            normalise(g)
+            transpose_pair(g)
+        quantise_pair(0)
+        normalise(3)
         kn_rows = keep.tile([P, K], BF16)
         nc.vector.tensor_scalar(
             out=kn_rows[:], in0=e[:], scalar1=e_inverse_length[:, 0:1], scalar2=None, op0=ALU.mult
         )
         kn_planes = psum_words.tile([P, HALVES, P], F32, tag="planes")
         transpose_words(nc, identity[:], kn_planes, kn_rows[:])
-        quantise_pair(1)
-        quantise_pair(2)
+        transpose_pair(3)
+        interleave(1, nc.vector.tensor_copy)
+        interleave(2, nc.scalar.copy)
+        interleave(3, nc.scalar.copy)
         kn_grouped = keep.tile([P, P * PACK], BF16, align_bytes=64)
         nc.vector.tensor_copy(
             out=kn_grouped[:].bitcast(F32).rearrange("p (r u) -> p r u", u=HALVES),
             in_=kn_planes[:].rearrange("p u r -> p r u"),
         )
-        quantise_pair(3)
+        quantise_pair(1)
         kn_codes = keep.tile([P, P], U32, align_bytes=64)
         kn_scales = keep.tile([P, P], U8, align_bytes=64)
         quantise(nc, kn_codes[:], kn_scales[:], kn_grouped[:])
+        quantise_pair(2)
+        quantise_pair(3)
 
         sims = []
-        sims_min_by_bank = keep.tile([P, SLOTS // BANK], F32)
         for b in range(SLOTS // BANK):
             bank_slots = slice(BANK * b, BANK * (b + 1))
             sims_bank = psum_sums.tile([P, BANK], F32, name="sims%d" % b)
@@ -219,29 +231,52 @@ def tile_contentaddressablewritehead_pa_s_kernel(tc, controller_output, Wk, bk, 
                 start=True,
                 stop=True,
             )
-            nc.vector.tensor_reduce(out=sims_min_by_bank[:, b : b + 1], in_=sims_bank[:], axis=AXIS_X, op=ALU.min)
             sims.append(sims_bank)
-        sims_min = keep.tile([P, 1], F32)
-        nc.vector.tensor_reduce(out=sims_min[:], in_=sims_min_by_bank[:], axis=AXIS_X, op=ALU.min)
         weights = keep.tile([P, SLOTS], F32)
-        sum_by_bank = keep.tile([P, SLOTS // BANK], F32)
-        for b in range(SLOTS // BANK):
-            nc.scalar.activation(
-                out=weights[:, BANK * b : BANK * (b + 1)],
-                in_=sims[b][:],
-                func=ACT.Exp,
-                bias=sims_min[:],
-                scale=-1.0,
-                accum_out=sum_by_bank[:, b : b + 1],
-            )
+        bank0_min = keep.tile([P, 1], F32)
+        nc.vector.tensor_reduce(out=bank0_min[:], in_=sims[0][:], axis=AXIS_X, op=ALU.min)
+        bank0_sum = keep.tile([P, 1], F32)
+        nc.scalar.activation(
+            out=weights[:, :BANK], in_=sims[0][:], func=ACT.Exp, bias=bank0_min[:], scale=-1.0, accum_out=bank0_sum[:]
+        )
+        sims1_copy = keep.tile([P, BANK], F32)
+        row_min = keep.tile([P, 1], F32)
+        nc.vector.tensor_scalar(
+            out=sims1_copy[:],
+            in0=sims[1][:],
+            scalar1=1.0,
+            scalar2=bank0_min[:, 0:1],
+            op0=ALU.mult,
+            op1=ALU.min,
+            accum_out=row_min[:],
+        )
+        bank1_sum = keep.tile([P, 1], F32)
+        nc.scalar.activation(
+            out=weights[:, BANK:], in_=sims[1][:], func=ACT.Exp, bias=row_min[:], scale=-1.0, accum_out=bank1_sum[:]
+        )
+        bank0_shift = keep.tile([P, 1], F32)
+        nc.vector.tensor_sub(out=bank0_shift[:], in0=row_min[:], in1=bank0_min[:])
+        bank0_factor = keep.tile([P, 1], F32)
+        nc.scalar.activation(out=bank0_factor[:], in_=bank0_shift[:], func=ACT.Exp)
         weight_sum = keep.tile([P, 1], F32)
-        nc.vector.tensor_reduce(out=weight_sum[:], in_=sum_by_bank[:], axis=AXIS_X, op=ALU.add)
-        inverse_sum = keep.tile([P, 1], F32)
-        nc.vector.reciprocal(out=inverse_sum[:], in_=weight_sum[:])
+        nc.vector.tensor_scalar(
+            out=weight_sum[:],
+            in0=bank0_sum[:],
+            scalar1=bank0_factor[:, 0:1],
+            scalar2=bank1_sum[:, 0:1],
+            op0=ALU.mult,
+            op1=ALU.add,
+        )
+        bank1_gain = keep.tile([P, 1], F32)
+        nc.vector.reciprocal(out=bank1_gain[:], in_=weight_sum[:])
+        bank0_gain = keep.tile([P, 1], F32)
+        nc.vector.tensor_mul(out=bank0_gain[:], in0=bank0_factor[:], in1=bank1_gain[:])
         out_rows = out.flatten_outer_dims()
-        for b in range(SLOTS // BANK):
-            bank_slots = slice(BANK * b, BANK * (b + 1))
-            nc.vector.tensor_scalar(
-                out=weights[:, bank_slots], in0=weights[:, bank_slots], scalar1=inverse_sum[:, 0:1], scalar2=None, op0=ALU.mult
-            )
-            nc.sync.dma_start(out=out_rows[:, bank_slots], in_=weights[:, bank_slots])
+        nc.vector.tensor_scalar(
+            out=weights[:, BANK:], in0=weights[:, BANK:], scalar1=bank1_gain[:, 0:1], scalar2=None, op0=ALU.mult
+        )
+        nc.sync.dma_start(out=out_rows[:, BANK:], in_=weights[:, BANK:])
+        nc.vector.tensor_scalar(
+            out=weights[:, :BANK], in0=weights[:, :BANK], scalar1=bank0_gain[:, 0:1], scalar2=None, op0=ALU.mult
+        )
+        nc.sync.dma_start(out=out_rows[:, :BANK], in_=weights[:, :BANK])

@@ -15,12 +15,15 @@ AXIS_X = mybir.AxisListType.X
 P = 128
 K = 512
 PACK = 4
+WORD = 2
 HALVES = 2
 SLOTS = 1024
-SLOT_TILES = SLOTS // P
-PAIRS = SLOT_TILES // 2
 BANK = 512
+PAIR = 2
+PAIRS = SLOTS // (PAIR * P)
+WORD_BANKS = 4
 NORM_FLOOR = 1e-12
+RUN = 4
 WK_VECTOR_COLS = 384
 
 FLOPS = 2 * P * K * K + 2 * P * K * SLOTS
@@ -42,30 +45,30 @@ def tile_contentaddressablewritehead_pa_s_kernel(tc, controller_output, Wk, bk, 
         const = ctx.enter_context(tc.tile_pool(name="const", bufs=1))
         keep = ctx.enter_context(tc.tile_pool(name="keep", bufs=1))
         pairs = ctx.enter_context(tc.tile_pool(name="pairs", bufs=PAIRS))
-        psum_words = ctx.enter_context(tc.psum_pool(name="psum_words", bufs=4))
+        psum_words = ctx.enter_context(tc.psum_pool(name="psum_words", bufs=WORD_BANKS))
         psum_sums = ctx.enter_context(tc.psum_pool(name="psum_sums", bufs=1))
         ctx.enter_context(tc.manual_schedule())
 
         memory_tiles = memory.rearrange("(j p) k -> p j k", p=P)
         memory_pairs = []
         for g in range(PAIRS):
-            memory_pair = pairs.tile([P, 2, K], BF16)
+            memory_pair = pairs.tile([P, PAIR, K], BF16)
             memory_pairs.append(memory_pair)
         wk_rows = keep.tile([P, PACK, K], BF16)
         x_rows = keep.tile([P, K], BF16)
         bias_rows = const.tile([P, K], BF16)
         nc.vector.memset(bias_rows[:], 0.0)
         nc.scalar.dma_start(out=bias_rows[0:1, :], in_=bk.rearrange("(o m) -> o m", o=1))
-        nc.sync.dma_start(out=memory_pairs[0][:], in_=memory_tiles[:, 0:2, :])
+        nc.sync.dma_start(out=memory_pairs[0][:], in_=memory_tiles[:, 0:PAIR, :])
         nc.sync.dma_start(
             out=wk_rows[:].rearrange("p (u e) c -> p u (e c)", u=HALVES),
-            in_=Wk.rearrange("(u p e) c -> p u (e c)", u=HALVES, e=2),
+            in_=Wk.rearrange("(u p e) c -> p u (e c)", u=HALVES, e=WORD),
         )
         nc.sync.dma_start(out=x_rows[:], in_=controller_output.flatten_outer_dims())
         for g in range(1, PAIRS):
-            nc.sync.dma_start(out=memory_pairs[g][:], in_=memory_tiles[:, 2 * g : 2 * g + 2, :])
+            nc.sync.dma_start(out=memory_pairs[g][:], in_=memory_tiles[:, PAIR * g : PAIR * (g + 1), :])
 
-        minus_half = const.tile([P, 2], F32)
+        minus_half = const.tile([P, PAIR], F32)
         nc.gpsimd.memset(minus_half[:], -0.5)
         identity = const.tile([P, P], F32)
         make_identity(nc, identity[:])
@@ -82,24 +85,24 @@ def tile_contentaddressablewritehead_pa_s_kernel(tc, controller_output, Wk, bk, 
         grouped_of_pair = []
 
         def measure(g):
-            squares = pairs.tile([P, 2, K], BF16)
-            sum_squares = pairs.tile([P, 2], F32)
-            for i in range(2):
+            squares = pairs.tile([P, PAIR, K], BF16)
+            sum_squares = pairs.tile([P, PAIR], F32)
+            for i in range(PAIR):
                 nc.scalar.activation(
                     out=squares[:, i, :],
                     in_=memory_pairs[g][:, i, :],
                     func=ACT.Square,
                     accum_out=sum_squares[:, i : i + 1],
                 )
-            floored = pairs.tile([P, 2], F32)
+            floored = pairs.tile([P, PAIR], F32)
             nc.gpsimd.tensor_scalar_max(out=floored[:], in0=sum_squares[:], scalar1=NORM_FLOOR)
-            inverse_length = pairs.tile([P, 2], F32)
+            inverse_length = pairs.tile([P, PAIR], F32)
             nc.gpsimd.tensor_tensor(out=inverse_length[:], in0=floored[:], in1=minus_half[:], op=ALU.pow)
             inverse_lengths.append(inverse_length)
 
         def normalise(g):
-            mn_rows = pairs.tile([P, 2, K], BF16)
-            for i in range(2):
+            mn_rows = pairs.tile([P, PAIR, K], BF16)
+            for i in range(PAIR):
                 nc.vector.tensor_scalar(
                     out=mn_rows[:, i, :],
                     in0=memory_pairs[g][:, i, :],
@@ -110,33 +113,33 @@ def tile_contentaddressablewritehead_pa_s_kernel(tc, controller_output, Wk, bk, 
             rows_of_pair.append(mn_rows)
 
         def transpose_pair(g):
-            mn_planes = psum_words.tile([P, 2, HALVES, P], F32, tag="planes")
-            for i in range(2):
+            mn_planes = psum_words.tile([P, PAIR, HALVES, P], F32, tag="planes")
+            for i in range(PAIR):
                 transpose_words(nc, identity[:], mn_planes[:, i, :, :], rows_of_pair[g][:, i, :])
             planes_of_pair.append(mn_planes)
 
         def interleave(g, copy):
-            mn_grouped = pairs.tile([P, 2 * P * PACK], BF16, align_bytes=64)
+            mn_grouped = pairs.tile([P, PAIR * P * PACK], BF16, align_bytes=64)
             copy(
-                out=mn_grouped[:].bitcast(F32).rearrange("p (i r u) -> p i r u", i=2, u=HALVES),
+                out=mn_grouped[:].bitcast(F32).rearrange("p (i r u) -> p i r u", i=PAIR, u=HALVES),
                 in_=planes_of_pair[g][:].rearrange("p i u r -> p i r u"),
             )
             grouped_of_pair.append(mn_grouped)
 
         def quantise_pair(g):
-            pair_slots = slice(2 * P * g, 2 * P * (g + 1))
+            pair_slots = slice(PAIR * P * g, PAIR * P * (g + 1))
             quantise(nc, mn_codes[:, pair_slots], mn_scales[:, pair_slots], grouped_of_pair[g][:])
 
         measure(0)
 
         wk_grouped = keep.tile([P, K, PACK], BF16, align_bytes=64)
         nc.vector.tensor_copy(
-            out=wk_grouped[:, :WK_VECTOR_COLS, :].rearrange("p (c i) t -> p c t i", i=4),
-            in_=wk_rows[:, :, :WK_VECTOR_COLS].rearrange("p t (c i) -> p c t i", i=4),
+            out=wk_grouped[:, :WK_VECTOR_COLS, :].rearrange("p (c i) t -> p c t i", i=RUN),
+            in_=wk_rows[:, :, :WK_VECTOR_COLS].rearrange("p t (c i) -> p c t i", i=RUN),
         )
         nc.scalar.copy(
-            out=wk_grouped[:, WK_VECTOR_COLS:, :].rearrange("p (c i) t -> p c t i", i=4),
-            in_=wk_rows[:, :, WK_VECTOR_COLS:].rearrange("p t (c i) -> p c t i", i=4),
+            out=wk_grouped[:, WK_VECTOR_COLS:, :].rearrange("p (c i) t -> p c t i", i=RUN),
+            in_=wk_rows[:, :, WK_VECTOR_COLS:].rearrange("p t (c i) -> p c t i", i=RUN),
         )
 
         x_planes = psum_words.tile([P, HALVES, P], F32, tag="planes")
@@ -191,18 +194,18 @@ def tile_contentaddressablewritehead_pa_s_kernel(tc, controller_output, Wk, bk, 
         nc.gpsimd.tensor_tensor(
             out=e_inverse_length[:], in0=e_sum_squares[:], in1=minus_half[:, 0:1], op=ALU.pow
         )
-        for g in (1, 2):
+        for g in range(1, PAIRS - 1):
             normalise(g)
             transpose_pair(g)
         quantise_pair(0)
-        normalise(3)
+        normalise(PAIRS - 1)
         kn_rows = keep.tile([P, K], BF16)
         nc.vector.tensor_scalar(
             out=kn_rows[:], in0=e[:], scalar1=e_inverse_length[:, 0:1], scalar2=None, op0=ALU.mult
         )
         kn_planes = psum_words.tile([P, HALVES, P], F32, tag="planes")
         transpose_words(nc, identity[:], kn_planes, kn_rows[:])
-        transpose_pair(3)
+        transpose_pair(PAIRS - 1)
         interleave(1, nc.vector.tensor_copy)
         interleave(2, nc.scalar.copy)
         interleave(3, nc.scalar.copy)
@@ -254,10 +257,8 @@ def tile_contentaddressablewritehead_pa_s_kernel(tc, controller_output, Wk, bk, 
         nc.scalar.activation(
             out=weights[:, BANK:], in_=sims[1][:], func=ACT.Exp, bias=row_min[:], scale=-1.0, accum_out=bank1_sum[:]
         )
-        bank0_shift = keep.tile([P, 1], F32)
-        nc.vector.tensor_sub(out=bank0_shift[:], in0=row_min[:], in1=bank0_min[:])
         bank0_factor = keep.tile([P, 1], F32)
-        nc.scalar.activation(out=bank0_factor[:], in_=bank0_shift[:], func=ACT.Exp)
+        nc.scalar.activation(out=bank0_factor[:], in_=bank0_min[:], func=ACT.Exp, bias=row_min[:], scale=-1.0)
         weight_sum = keep.tile([P, 1], F32)
         nc.vector.tensor_scalar(
             out=weight_sum[:],

@@ -24,7 +24,6 @@ PAIRS = SLOTS // (PAIR * P)
 WORD_BANKS = 4
 NORM_FLOOR = 1e-12
 RUN = 4
-WK_VECTOR_COLS = 384
 
 FLOPS = 2 * P * K * K + 2 * P * K * SLOTS
 
@@ -57,8 +56,8 @@ def tile_contentaddressablewritehead_pa_s_kernel(tc, controller_output, Wk, bk, 
         wk_rows = keep.tile([P, PACK, K], BF16)
         x_rows = keep.tile([P, K], BF16)
         bias_rows = const.tile([P, K], BF16)
-        nc.vector.memset(bias_rows[:], 0.0)
-        nc.scalar.dma_start(out=bias_rows[0:1, :], in_=bk.rearrange("(o m) -> o m", o=1))
+        nc.gpsimd.memset(bias_rows[:], 0.0)
+        nc.gpsimd.dma_start(out=bias_rows[0:1, :], in_=bk.rearrange("(o m) -> o m", o=1))
         nc.sync.dma_start(out=memory_pairs[0][:], in_=memory_tiles[:, 0:PAIR, :])
         nc.sync.dma_start(
             out=wk_rows[:].rearrange("p (u e) c -> p u (e c)", u=HALVES),
@@ -69,7 +68,7 @@ def tile_contentaddressablewritehead_pa_s_kernel(tc, controller_output, Wk, bk, 
             nc.sync.dma_start(out=memory_pairs[g][:], in_=memory_tiles[:, PAIR * g : PAIR * (g + 1), :])
 
         minus_half = const.tile([P, PAIR], F32)
-        nc.gpsimd.memset(minus_half[:], -0.5)
+        nc.vector.memset(minus_half[:], -0.5)
         identity = const.tile([P, P], F32)
         make_identity(nc, identity[:])
         ones = const.tile([P, P], BF16)
@@ -134,18 +133,14 @@ def tile_contentaddressablewritehead_pa_s_kernel(tc, controller_output, Wk, bk, 
 
         wk_grouped = keep.tile([P, K, PACK], BF16, align_bytes=64)
         nc.vector.tensor_copy(
-            out=wk_grouped[:, :WK_VECTOR_COLS, :].rearrange("p (c i) t -> p c t i", i=RUN),
-            in_=wk_rows[:, :, :WK_VECTOR_COLS].rearrange("p t (c i) -> p c t i", i=RUN),
-        )
-        nc.scalar.copy(
-            out=wk_grouped[:, WK_VECTOR_COLS:, :].rearrange("p (c i) t -> p c t i", i=RUN),
-            in_=wk_rows[:, :, WK_VECTOR_COLS:].rearrange("p t (c i) -> p c t i", i=RUN),
+            out=wk_grouped[:].rearrange("p (c i) t -> p c t i", i=RUN),
+            in_=wk_rows[:].rearrange("p t (c i) -> p c t i", i=RUN),
         )
 
         x_planes = psum_words.tile([P, HALVES, P], F32, tag="planes")
         transpose_words(nc, identity[:], x_planes, x_rows[:])
         x_grouped = keep.tile([P, P * PACK], BF16, align_bytes=64)
-        nc.scalar.copy(
+        nc.vector.tensor_copy(
             out=x_grouped[:].bitcast(F32).rearrange("p (r u) -> p r u", u=HALVES),
             in_=x_planes[:].rearrange("p u r -> p r u"),
         )
@@ -178,11 +173,14 @@ def tile_contentaddressablewritehead_pa_s_kernel(tc, controller_output, Wk, bk, 
         z = keep.tile([P, K], F32)
         nc.vector.tensor_tensor(out=z[:], in0=z_sum[:], in1=bias[:], op=ALU.add)
 
-        minus_max = keep.tile([P, 1], F32)
-        nc.vector.tensor_reduce(out=minus_max[:], in_=z[:], axis=AXIS_X, op=ALU.max, negate=True)
-        interleave(0, nc.vector.tensor_copy)
+        minus_2z = keep.tile([P, K], F32)
         minus_2max = keep.tile([P, 1], F32)
-        nc.vector.tensor_scalar_mul(out=minus_2max[:], in0=minus_max[:], scalar1=2.0)
+        nc.vector.tensor_scalar(
+            out=minus_2z[:], in0=z[:], scalar1=-2.0, scalar2=None, op0=ALU.mult, op1=ALU.min, accum_out=minus_2max[:]
+        )
+        interleave(0, nc.vector.tensor_copy)
+        minus_max = keep.tile([P, 1], F32)
+        nc.vector.tensor_scalar_mul(out=minus_max[:], in0=minus_2max[:], scalar1=0.5)
         e_squared = keep.tile([P, K], BF16)
         e_sum_squares = keep.tile([P, 1], F32)
         nc.scalar.activation(
@@ -194,18 +192,16 @@ def tile_contentaddressablewritehead_pa_s_kernel(tc, controller_output, Wk, bk, 
         nc.gpsimd.tensor_tensor(
             out=e_inverse_length[:], in0=e_sum_squares[:], in1=minus_half[:, 0:1], op=ALU.pow
         )
-        for g in range(1, PAIRS - 1):
+        for g in range(1, PAIRS):
             normalise(g)
             transpose_pair(g)
-        quantise_pair(0)
-        normalise(PAIRS - 1)
         kn_rows = keep.tile([P, K], BF16)
         nc.vector.tensor_scalar(
             out=kn_rows[:], in0=e[:], scalar1=e_inverse_length[:, 0:1], scalar2=None, op0=ALU.mult
         )
         kn_planes = psum_words.tile([P, HALVES, P], F32, tag="planes")
         transpose_words(nc, identity[:], kn_planes, kn_rows[:])
-        transpose_pair(PAIRS - 1)
+        quantise_pair(0)
         interleave(1, nc.vector.tensor_copy)
         interleave(2, nc.scalar.copy)
         interleave(3, nc.scalar.copy)

@@ -49,55 +49,67 @@ def tile_contentaddressablewritehead_pa_s_kernel(tc, controller_output, Wk, bk, 
         ctx.enter_context(tc.manual_schedule())
 
         memory_tiles = memory.rearrange("(j p) k -> p j k", p=P)
+        out_rows = out.flatten_outer_dims()
         memory_pairs = []
+        sums_of_pair = []
         for g in range(PAIRS):
             memory_pair = pairs.tile([P, PAIR, K], BF16)
             memory_pairs.append(memory_pair)
+            sum_squares = pairs.tile([P, PAIR], F32)
+            sums_of_pair.append(sum_squares)
         wk_rows = keep.tile([P, PACK, K], BF16)
         x_rows = keep.tile([P, K], BF16)
         bias_rows = const.tile([P, K], BF16)
-        nc.gpsimd.memset(bias_rows[:], 0.0)
-        nc.gpsimd.dma_start(out=bias_rows[0:1, :], in_=bk.rearrange("(o m) -> o m", o=1))
-        nc.sync.dma_start(out=memory_pairs[0][:], in_=memory_tiles[:, 0:PAIR, :])
-        nc.sync.dma_start(
-            out=wk_rows[:].rearrange("p (u e) c -> p u (e c)", u=HALVES),
-            in_=Wk.rearrange("(u p e) c -> p u (e c)", u=HALVES, e=WORD),
-        )
-        nc.sync.dma_start(out=x_rows[:], in_=controller_output.flatten_outer_dims())
-        for g in range(1, PAIRS):
-            nc.sync.dma_start(out=memory_pairs[g][:], in_=memory_tiles[:, PAIR * g : PAIR * (g + 1), :])
-
         minus_half = const.tile([P, PAIR], F32)
-        nc.vector.memset(minus_half[:], -0.5)
         identity = const.tile([P, P], F32)
-        make_identity(nc, identity[:])
         ones = const.tile([P, P], BF16)
-        nc.vector.memset(ones[:], 1.0)
         table_warmer = const.tile([P, 1], F32)
-        nc.scalar.activation(out=table_warmer[:], in_=minus_half[:, 0:1], func=ACT.Exp)
-
         mn_codes = keep.tile([P, SLOTS], U32, align_bytes=64)
         mn_scales = keep.tile([P, SLOTS], U8, align_bytes=64)
-        inverse_lengths = []
-        rows_of_pair = []
-        planes_of_pair = []
-        grouped_of_pair = []
+        inverse_lengths = {}
+        rows_of_pair = {}
+        planes_of_pair = {}
+        grouped_of_pair = {}
 
-        def measure(g):
-            squares = pairs.tile([P, PAIR, K], BF16)
-            sum_squares = pairs.tile([P, PAIR], F32)
-            for i in range(PAIR):
-                nc.scalar.activation(
-                    out=squares[:, i, :],
-                    in_=memory_pairs[g][:, i, :],
-                    func=ACT.Square,
-                    accum_out=sum_squares[:, i : i + 1],
-                )
+        def load_memory(g):
+            nc.sync.dma_start(out=memory_pairs[g][:], in_=memory_tiles[:, PAIR * g : PAIR * (g + 1), :])
+
+        def load_wk():
+            nc.sync.dma_start(
+                out=wk_rows[:].rearrange("p (u e) c -> p u (e c)", u=HALVES),
+                in_=Wk.rearrange("(u p e) c -> p u (e c)", u=HALVES, e=WORD),
+            )
+
+        def load_x():
+            nc.sync.dma_start(out=x_rows[:], in_=controller_output.flatten_outer_dims())
+
+        def square_scalar(g, i):
+            squares = pairs.tile([P, K], BF16, tag="squares_s")
+            nc.scalar.activation(
+                out=squares[:],
+                in_=memory_pairs[g][:, i, :],
+                func=ACT.Square,
+                accum_out=sums_of_pair[g][:, i : i + 1],
+            )
+
+        def square_vector(g, i):
+            squares = pairs.tile([P, K], F32, tag="squares_v")
+            nc.vector.scalar_tensor_tensor(
+                out=squares[:],
+                in0=memory_pairs[g][:, i, :],
+                scalar=1.0,
+                in1=memory_pairs[g][:, i, :],
+                op0=ALU.mult,
+                op1=ALU.mult,
+                accum_out=sums_of_pair[g][:, i : i + 1],
+            )
+
+        def root(g):
             floored = pairs.tile([P, PAIR], F32)
-            nc.gpsimd.tensor_scalar_max(out=floored[:], in0=sum_squares[:], scalar1=NORM_FLOOR)
+            nc.gpsimd.tensor_scalar_max(out=floored[:], in0=sums_of_pair[g][:], scalar1=NORM_FLOOR)
             inverse_length = pairs.tile([P, PAIR], F32)
             nc.gpsimd.tensor_tensor(out=inverse_length[:], in0=floored[:], in1=minus_half[:], op=ALU.pow)
-            inverse_lengths.append(inverse_length)
+            inverse_lengths[g] = inverse_length
 
         def normalise(g):
             mn_rows = pairs.tile([P, PAIR, K], BF16)
@@ -109,13 +121,13 @@ def tile_contentaddressablewritehead_pa_s_kernel(tc, controller_output, Wk, bk, 
                     scalar2=None,
                     op0=ALU.mult,
                 )
-            rows_of_pair.append(mn_rows)
+            rows_of_pair[g] = mn_rows
 
         def transpose_pair(g):
             mn_planes = psum_words.tile([P, PAIR, HALVES, P], F32, tag="planes")
             for i in range(PAIR):
                 transpose_words(nc, identity[:], mn_planes[:, i, :, :], rows_of_pair[g][:, i, :])
-            planes_of_pair.append(mn_planes)
+            planes_of_pair[g] = mn_planes
 
         def interleave(g, copy):
             mn_grouped = pairs.tile([P, PAIR * P * PACK], BF16, align_bytes=64)
@@ -123,96 +135,125 @@ def tile_contentaddressablewritehead_pa_s_kernel(tc, controller_output, Wk, bk, 
                 out=mn_grouped[:].bitcast(F32).rearrange("p (i r u) -> p i r u", i=PAIR, u=HALVES),
                 in_=planes_of_pair[g][:].rearrange("p i u r -> p i r u"),
             )
-            grouped_of_pair.append(mn_grouped)
+            grouped_of_pair[g] = mn_grouped
 
         def quantise_pair(g):
             pair_slots = slice(PAIR * P * g, PAIR * P * (g + 1))
             quantise(nc, mn_codes[:, pair_slots], mn_scales[:, pair_slots], grouped_of_pair[g][:])
 
-        measure(0)
-
         wk_grouped = keep.tile([P, K, PACK], BF16, align_bytes=64)
-        nc.vector.tensor_copy(
-            out=wk_grouped[:].rearrange("p (c i) t -> p c t i", i=RUN),
-            in_=wk_rows[:].rearrange("p t (c i) -> p c t i", i=RUN),
-        )
-
-        x_planes = psum_words.tile([P, HALVES, P], F32, tag="planes")
-        transpose_words(nc, identity[:], x_planes, x_rows[:])
         x_grouped = keep.tile([P, P * PACK], BF16, align_bytes=64)
-        nc.vector.tensor_copy(
-            out=x_grouped[:].bitcast(F32).rearrange("p (r u) -> p r u", u=HALVES),
-            in_=x_planes[:].rearrange("p u r -> p r u"),
-        )
         wk_codes = keep.tile([P, K], U32, align_bytes=64)
         wk_scales = keep.tile([P, K], U8, align_bytes=64)
-        quantise(nc, wk_codes[:], wk_scales[:], wk_grouped[:].rearrange("p c t -> p (c t)"))
         x_codes = keep.tile([P, P], U32, align_bytes=64)
         x_scales = keep.tile([P, P], U8, align_bytes=64)
-        quantise(nc, x_codes[:], x_scales[:], x_grouped[:])
-
-        bias_sum = psum_sums.tile([P, K], F32)
-        nc.tensor.matmul(out=bias_sum[:], lhsT=ones[:], rhs=bias_rows[:], start=True, stop=True)
         bias = const.tile([P, K], F32)
-        nc.vector.tensor_copy(out=bias[:], in_=bias_sum[:])
-
-        z_sum = psum_sums.tile([P, K], F32)
-        nc.tensor.matmul_mx(
-            out=z_sum[:],
-            lhsT=x_codes[:].bitcast(FP8X4),
-            lhsT_scale=x_scales[:],
-            rhs=wk_codes[:].bitcast(FP8X4),
-            rhs_scale=wk_scales[:],
-            start=True,
-            stop=True,
-        )
-        for g in range(1, PAIRS):
-            measure(g)
-        normalise(0)
-        transpose_pair(0)
         z = keep.tile([P, K], F32)
-        nc.vector.tensor_tensor(out=z[:], in0=z_sum[:], in1=bias[:], op=ALU.add)
-
         minus_2z = keep.tile([P, K], F32)
         minus_2max = keep.tile([P, 1], F32)
+        minus_max = keep.tile([P, 1], F32)
+        e_squared = keep.tile([P, K], BF16)
+        e_sum_squares = keep.tile([P, 1], F32)
+        e = keep.tile([P, K], F32)
+        e_inverse_length = keep.tile([P, 1], F32)
+        kn_rows = keep.tile([P, K], BF16)
+        kn_grouped = keep.tile([P, P * PACK], BF16, align_bytes=64)
+        kn_codes = keep.tile([P, P], U32, align_bytes=64)
+        kn_scales = keep.tile([P, P], U8, align_bytes=64)
+        weights = keep.tile([P, SLOTS], F32)
+
+        def regroup_wk():
+            nc.vector.tensor_copy(
+                out=wk_grouped[:].rearrange("p (c i) t -> p c t i", i=RUN),
+                in_=wk_rows[:].rearrange("p t (c i) -> p c t i", i=RUN),
+            )
+
+        def copy_words(copy, grouped, planes):
+            copy(
+                out=grouped[:].bitcast(F32).rearrange("p (r u) -> p r u", u=HALVES),
+                in_=planes[:].rearrange("p u r -> p r u"),
+            )
+
+        def multiply(sums, lhs_codes, lhs_scales, rhs_codes, rhs_scales):
+            nc.tensor.matmul_mx(
+                out=sums,
+                lhsT=lhs_codes.bitcast(FP8X4),
+                lhsT_scale=lhs_scales,
+                rhs=rhs_codes.bitcast(FP8X4),
+                rhs_scale=rhs_scales,
+                start=True,
+                stop=True,
+            )
+
+        nc.gpsimd.memset(bias_rows[:], 0.0)
+        nc.gpsimd.dma_start(out=bias_rows[0:1, :], in_=bk.rearrange("(o m) -> o m", o=1))
+        load_memory(0)
+        load_wk()
+        load_x()
+        for g in range(1, PAIRS):
+            load_memory(g)
+
+        nc.vector.memset(minus_half[:], -0.5)
+        make_identity(nc, identity[:])
+        nc.vector.memset(ones[:], 1.0)
+        nc.scalar.activation(out=table_warmer[:], in_=minus_half[:, 0:1], func=ACT.Exp)
+
+        square_scalar(0, 0)
+        square_scalar(0, 1)
+        root(0)
+        regroup_wk()
+        x_planes = psum_words.tile([P, HALVES, P], F32, tag="planes")
+        transpose_words(nc, identity[:], x_planes, x_rows[:])
+        copy_words(nc.vector.tensor_copy, x_grouped, x_planes)
+        quantise(nc, wk_codes[:], wk_scales[:], wk_grouped[:].rearrange("p c t -> p (c t)"))
+        quantise(nc, x_codes[:], x_scales[:], x_grouped[:])
+        bias_sum = psum_sums.tile([P, K], F32)
+        nc.tensor.matmul(out=bias_sum[:], lhsT=ones[:], rhs=bias_rows[:], start=True, stop=True)
+        nc.vector.tensor_copy(out=bias[:], in_=bias_sum[:])
+        z_sum = psum_sums.tile([P, K], F32)
+        multiply(z_sum[:], x_codes[:], x_scales[:], wk_codes[:], wk_scales[:])
+        for g in range(1, PAIRS):
+            square_scalar(g, 0)
+            square_scalar(g, 1)
+            root(g)
+        normalise(0)
+        transpose_pair(0)
+        nc.vector.tensor_tensor(out=z[:], in0=z_sum[:], in1=bias[:], op=ALU.add)
+
         nc.vector.tensor_scalar(
             out=minus_2z[:], in0=z[:], scalar1=-2.0, scalar2=None, op0=ALU.mult, op1=ALU.min, accum_out=minus_2max[:]
         )
+
         interleave(0, nc.vector.tensor_copy)
-        minus_max = keep.tile([P, 1], F32)
         nc.vector.tensor_scalar_mul(out=minus_max[:], in0=minus_2max[:], scalar1=0.5)
-        e_squared = keep.tile([P, K], BF16)
-        e_sum_squares = keep.tile([P, 1], F32)
+
         nc.scalar.activation(
             out=e_squared[:], in_=z[:], func=ACT.Exp, bias=minus_2max[:], scale=2.0, accum_out=e_sum_squares[:]
         )
-        e = keep.tile([P, K], F32)
         nc.scalar.activation(out=e[:], in_=z[:], func=ACT.Exp, bias=minus_max[:], scale=1.0)
-        e_inverse_length = keep.tile([P, 1], F32)
         nc.gpsimd.tensor_tensor(
             out=e_inverse_length[:], in0=e_sum_squares[:], in1=minus_half[:, 0:1], op=ALU.pow
         )
-        for g in range(1, PAIRS):
-            normalise(g)
-            transpose_pair(g)
-        kn_rows = keep.tile([P, K], BF16)
+
+        normalise(1)
+        transpose_pair(1)
+        normalise(2)
+        transpose_pair(2)
+        normalise(3)
+
         nc.vector.tensor_scalar(
             out=kn_rows[:], in0=e[:], scalar1=e_inverse_length[:, 0:1], scalar2=None, op0=ALU.mult
         )
         kn_planes = psum_words.tile([P, HALVES, P], F32, tag="planes")
         transpose_words(nc, identity[:], kn_planes, kn_rows[:])
+
+        transpose_pair(3)
         quantise_pair(0)
-        interleave(1, nc.vector.tensor_copy)
+        interleave(1, nc.scalar.copy)
         interleave(2, nc.scalar.copy)
+        copy_words(nc.vector.tensor_copy, kn_grouped, kn_planes)
         interleave(3, nc.scalar.copy)
-        kn_grouped = keep.tile([P, P * PACK], BF16, align_bytes=64)
-        nc.vector.tensor_copy(
-            out=kn_grouped[:].bitcast(F32).rearrange("p (r u) -> p r u", u=HALVES),
-            in_=kn_planes[:].rearrange("p u r -> p r u"),
-        )
         quantise_pair(1)
-        kn_codes = keep.tile([P, P], U32, align_bytes=64)
-        kn_scales = keep.tile([P, P], U8, align_bytes=64)
         quantise(nc, kn_codes[:], kn_scales[:], kn_grouped[:])
         quantise_pair(2)
         quantise_pair(3)
@@ -221,17 +262,8 @@ def tile_contentaddressablewritehead_pa_s_kernel(tc, controller_output, Wk, bk, 
         for b in range(SLOTS // BANK):
             bank_slots = slice(BANK * b, BANK * (b + 1))
             sims_bank = psum_sums.tile([P, BANK], F32, name="sims%d" % b)
-            nc.tensor.matmul_mx(
-                out=sims_bank[:],
-                lhsT=kn_codes[:].bitcast(FP8X4),
-                lhsT_scale=kn_scales[:],
-                rhs=mn_codes[:, bank_slots].bitcast(FP8X4),
-                rhs_scale=mn_scales[:, bank_slots],
-                start=True,
-                stop=True,
-            )
+            multiply(sims_bank[:], kn_codes[:], kn_scales[:], mn_codes[:, bank_slots], mn_scales[:, bank_slots])
             sims.append(sims_bank)
-        weights = keep.tile([P, SLOTS], F32)
         bank0_min = keep.tile([P, 1], F32)
         nc.vector.tensor_reduce(out=bank0_min[:], in_=sims[0][:], axis=AXIS_X, op=ALU.min)
         bank0_sum = keep.tile([P, 1], F32)
@@ -268,7 +300,6 @@ def tile_contentaddressablewritehead_pa_s_kernel(tc, controller_output, Wk, bk, 
         nc.vector.reciprocal(out=bank1_gain[:], in_=weight_sum[:])
         bank0_gain = keep.tile([P, 1], F32)
         nc.vector.tensor_mul(out=bank0_gain[:], in0=bank0_factor[:], in1=bank1_gain[:])
-        out_rows = out.flatten_outer_dims()
         nc.vector.tensor_scalar(
             out=weights[:, BANK:], in0=weights[:, BANK:], scalar1=bank1_gain[:, 0:1], scalar2=None, op0=ALU.mult
         )

@@ -23,6 +23,8 @@ PAIR = 2
 PAIRS = SLOTS // (PAIR * P)
 WORD_BANKS = 4
 NORM_FLOOR = 1e-12
+PART = PAIR * P
+SIMS_BANKS = ("bias_sum", "z_sum", "sims_a", "sims_b")
 RUN = 4
 
 FLOPS = 2 * P * K * K + 2 * P * K * SLOTS
@@ -258,53 +260,52 @@ def tile_contentaddressablewritehead_pa_s_kernel(tc, controller_output, Wk, bk, 
         quantise_pair(2)
         quantise_pair(3)
 
+        part_min = keep.tile([P, PAIRS], F32)
+        part_sum = keep.tile([P, PAIRS], F32)
         sims = []
-        for b in range(SLOTS // BANK):
-            bank_slots = slice(BANK * b, BANK * (b + 1))
-            sims_bank = psum_sums.tile([P, BANK], F32, name="sims%d" % b)
-            multiply(sims_bank[:], kn_codes[:], kn_scales[:], mn_codes[:, bank_slots], mn_scales[:, bank_slots])
-            sims.append(sims_bank)
-        bank0_min = keep.tile([P, 1], F32)
-        nc.vector.tensor_reduce(out=bank0_min[:], in_=sims[0][:], axis=AXIS_X, op=ALU.min)
-        bank0_sum = keep.tile([P, 1], F32)
-        nc.scalar.activation(
-            out=weights[:, :BANK], in_=sims[0][:], func=ACT.Exp, bias=bank0_min[:], scale=-1.0, accum_out=bank0_sum[:]
-        )
-        sims1_copy = keep.tile([P, BANK], F32)
+        for g in range(PAIRS):
+            part = slice(PART * g, PART * (g + 1))
+            sims_part = psum_sums.tile([P, BANK], F32, tag=SIMS_BANKS[g])
+            multiply(sims_part[:, :PART], kn_codes[:], kn_scales[:], mn_codes[:, part], mn_scales[:, part])
+            sims.append(sims_part)
+        for g in range(PAIRS):
+            part = slice(PART * g, PART * (g + 1))
+            nc.vector.tensor_reduce(out=part_min[:, g : g + 1], in_=sims[g][:, :PART], axis=AXIS_X, op=ALU.min)
+            nc.scalar.activation(
+                out=weights[:, part],
+                in_=sims[g][:, :PART],
+                func=ACT.Exp,
+                bias=part_min[:, g : g + 1],
+                scale=-1.0,
+                accum_out=part_sum[:, g : g + 1],
+            )
         row_min = keep.tile([P, 1], F32)
-        nc.vector.tensor_scalar(
-            out=sims1_copy[:],
-            in0=sims[1][:],
-            scalar1=1.0,
-            scalar2=bank0_min[:, 0:1],
+        nc.vector.tensor_reduce(out=row_min[:], in_=part_min[:], axis=AXIS_X, op=ALU.min)
+        factors = keep.tile([P, PAIRS], F32)
+        nc.scalar.activation(out=factors[:], in_=part_min[:], func=ACT.Exp, bias=row_min[:], scale=-1.0)
+        scaled_sums = keep.tile([P, PAIRS], F32)
+        row_sum = keep.tile([P, 1], F32)
+        nc.vector.scalar_tensor_tensor(
+            out=scaled_sums[:],
+            in0=factors[:],
+            scalar=1.0,
+            in1=part_sum[:],
             op0=ALU.mult,
-            op1=ALU.min,
-            accum_out=row_min[:],
+            op1=ALU.mult,
+            accum_out=row_sum[:],
         )
-        bank1_sum = keep.tile([P, 1], F32)
-        nc.scalar.activation(
-            out=weights[:, BANK:], in_=sims[1][:], func=ACT.Exp, bias=row_min[:], scale=-1.0, accum_out=bank1_sum[:]
-        )
-        bank0_factor = keep.tile([P, 1], F32)
-        nc.scalar.activation(out=bank0_factor[:], in_=bank0_min[:], func=ACT.Exp, bias=row_min[:], scale=-1.0)
-        weight_sum = keep.tile([P, 1], F32)
-        nc.vector.tensor_scalar(
-            out=weight_sum[:],
-            in0=bank0_sum[:],
-            scalar1=bank0_factor[:, 0:1],
-            scalar2=bank1_sum[:, 0:1],
-            op0=ALU.mult,
-            op1=ALU.add,
-        )
-        bank1_gain = keep.tile([P, 1], F32)
-        nc.vector.reciprocal(out=bank1_gain[:], in_=weight_sum[:])
-        bank0_gain = keep.tile([P, 1], F32)
-        nc.vector.tensor_mul(out=bank0_gain[:], in0=bank0_factor[:], in1=bank1_gain[:])
-        nc.vector.tensor_scalar(
-            out=weights[:, BANK:], in0=weights[:, BANK:], scalar1=bank1_gain[:, 0:1], scalar2=None, op0=ALU.mult
-        )
-        nc.sync.dma_start(out=out_rows[:, BANK:], in_=weights[:, BANK:])
-        nc.vector.tensor_scalar(
-            out=weights[:, :BANK], in0=weights[:, :BANK], scalar1=bank0_gain[:, 0:1], scalar2=None, op0=ALU.mult
-        )
-        nc.sync.dma_start(out=out_rows[:, :BANK], in_=weights[:, :BANK])
+        inverse_sum = keep.tile([P, 1], F32)
+        nc.vector.reciprocal(out=inverse_sum[:], in_=row_sum[:])
+        for b in reversed(range(SLOTS // BANK)):
+            for g in reversed(range(BANK // PART * b, BANK // PART * (b + 1))):
+                part = slice(PART * g, PART * (g + 1))
+                nc.vector.tensor_scalar(
+                    out=weights[:, part],
+                    in0=weights[:, part],
+                    scalar1=factors[:, g : g + 1],
+                    scalar2=inverse_sum[:, 0:1],
+                    op0=ALU.mult,
+                    op1=ALU.mult,
+                )
+            bank_slots = slice(BANK * b, BANK * (b + 1))
+            nc.sync.dma_start(out=out_rows[:, bank_slots], in_=weights[:, bank_slots])

@@ -21,6 +21,7 @@ SLOTS = 1024
 BANK = 512
 PAIR = 2
 PAIRS = SLOTS // (PAIR * P)
+TILES = SLOTS // P
 WORD_BANKS = 4
 NORM_FLOOR = 1e-12
 PART = PAIR * P
@@ -53,22 +54,21 @@ def tile_contentaddressablewritehead_pa_s_kernel(tc, controller_output, Wk, bk, 
         memory_tiles = memory.rearrange("(j p) k -> p j k", p=P)
         out_rows = out.flatten_outer_dims()
         memory_pairs = []
-        sums_of_pair = []
         for g in range(PAIRS):
             memory_pair = pairs.tile([P, PAIR, K], BF16)
             memory_pairs.append(memory_pair)
-            sum_squares = pairs.tile([P, PAIR], F32)
-            sums_of_pair.append(sum_squares)
         wk_rows = keep.tile([P, PACK, K], BF16)
         x_rows = keep.tile([P, K], BF16)
         bias_rows = const.tile([P, K], BF16)
-        minus_half = const.tile([P, PAIR], F32)
+        minus_half = const.tile([P, TILES], F32)
+        sum_squares = keep.tile([P, TILES], F32)
+        floored = keep.tile([P, TILES], F32)
+        inverse_length = keep.tile([P, TILES], F32)
         identity = const.tile([P, P], F32)
         ones = const.tile([P, P], BF16)
         table_warmer = const.tile([P, 1], F32)
         mn_codes = keep.tile([P, SLOTS], U32, align_bytes=64)
         mn_scales = keep.tile([P, SLOTS], U8, align_bytes=64)
-        inverse_lengths = {}
         rows_of_pair = {}
         planes_of_pair = {}
         grouped_of_pair = {}
@@ -91,7 +91,7 @@ def tile_contentaddressablewritehead_pa_s_kernel(tc, controller_output, Wk, bk, 
                 out=squares[:],
                 in_=memory_pairs[g][:, i, :],
                 func=ACT.Square,
-                accum_out=sums_of_pair[g][:, i : i + 1],
+                accum_out=sum_squares[:, PAIR * g + i : PAIR * g + i + 1],
             )
 
         def square_vector(g, i):
@@ -103,15 +103,15 @@ def tile_contentaddressablewritehead_pa_s_kernel(tc, controller_output, Wk, bk, 
                 in1=memory_pairs[g][:, i, :],
                 op0=ALU.mult,
                 op1=ALU.mult,
-                accum_out=sums_of_pair[g][:, i : i + 1],
+                accum_out=sum_squares[:, PAIR * g + i : PAIR * g + i + 1],
             )
 
-        def root(g):
-            floored = pairs.tile([P, PAIR], F32)
-            nc.gpsimd.tensor_scalar_max(out=floored[:], in0=sums_of_pair[g][:], scalar1=NORM_FLOOR)
-            inverse_length = pairs.tile([P, PAIR], F32)
-            nc.gpsimd.tensor_tensor(out=inverse_length[:], in0=floored[:], in1=minus_half[:], op=ALU.pow)
-            inverse_lengths[g] = inverse_length
+        def root(first, last):
+            tiles = slice(PAIR * first, PAIR * (last + 1))
+            nc.gpsimd.tensor_scalar_max(out=floored[:, tiles], in0=sum_squares[:, tiles], scalar1=NORM_FLOOR)
+            nc.gpsimd.tensor_tensor(
+                out=inverse_length[:, tiles], in0=floored[:, tiles], in1=minus_half[:, tiles], op=ALU.pow
+            )
 
         def normalise(g):
             mn_rows = pairs.tile([P, PAIR, K], BF16)
@@ -119,7 +119,7 @@ def tile_contentaddressablewritehead_pa_s_kernel(tc, controller_output, Wk, bk, 
                 nc.vector.tensor_scalar(
                     out=mn_rows[:, i, :],
                     in0=memory_pairs[g][:, i, :],
-                    scalar1=inverse_lengths[g][:, i : i + 1],
+                    scalar1=inverse_length[:, PAIR * g + i : PAIR * g + i + 1],
                     scalar2=None,
                     op0=ALU.mult,
                 )
@@ -187,8 +187,8 @@ def tile_contentaddressablewritehead_pa_s_kernel(tc, controller_output, Wk, bk, 
                 stop=True,
             )
 
-        nc.gpsimd.memset(bias_rows[:], 0.0)
-        nc.gpsimd.dma_start(out=bias_rows[0:1, :], in_=bk.rearrange("(o m) -> o m", o=1))
+        nc.vector.memset(bias_rows[:], 0.0)
+        nc.scalar.dma_start(out=bias_rows[0:1, :], in_=bk.rearrange("(o m) -> o m", o=1))
         load_memory(0)
         load_wk()
         load_x()
@@ -202,7 +202,7 @@ def tile_contentaddressablewritehead_pa_s_kernel(tc, controller_output, Wk, bk, 
 
         square_scalar(0, 0)
         square_scalar(0, 1)
-        root(0)
+        root(0, 0)
         regroup_wk()
         x_planes = psum_words.tile([P, HALVES, P], F32, tag="planes")
         transpose_words(nc, identity[:], x_planes, x_rows[:])
@@ -214,10 +214,13 @@ def tile_contentaddressablewritehead_pa_s_kernel(tc, controller_output, Wk, bk, 
         nc.vector.tensor_copy(out=bias[:], in_=bias_sum[:])
         z_sum = psum_sums.tile([P, K], F32)
         multiply(z_sum[:], x_codes[:], x_scales[:], wk_codes[:], wk_scales[:])
-        for g in range(1, PAIRS):
+        square_scalar(1, 0)
+        square_scalar(1, 1)
+        root(1, 1)
+        for g in range(2, PAIRS):
             square_scalar(g, 0)
             square_scalar(g, 1)
-            root(g)
+        root(2, PAIRS - 1)
         normalise(0)
         transpose_pair(0)
         nc.vector.tensor_tensor(out=z[:], in0=z_sum[:], in1=bias[:], op=ALU.add)

@@ -188,10 +188,10 @@ def tile_contentaddressablewritehead_pa_s_kernel(tc, controller_output, Wk, bk, 
             )
 
         nc.vector.memset(bias_rows[:], 0.0)
-        nc.scalar.dma_start(out=bias_rows[0:1, :], in_=bk.rearrange("(o m) -> o m", o=1))
         load_memory(0)
         load_wk()
         load_x()
+        nc.sync.dma_start(out=bias_rows[0:1, :], in_=bk.rearrange("(o m) -> o m", o=1))
         for g in range(1, PAIRS):
             load_memory(g)
 
@@ -207,50 +207,62 @@ def tile_contentaddressablewritehead_pa_s_kernel(tc, controller_output, Wk, bk, 
         x_planes = psum_words.tile([P, HALVES, P], F32, tag="planes")
         transpose_words(nc, identity[:], x_planes, x_rows[:])
         copy_words(nc.vector.tensor_copy, x_grouped, x_planes)
-        quantise(nc, wk_codes[:], wk_scales[:], wk_grouped[:].rearrange("p c t -> p (c t)"))
+        wk_flat = wk_grouped[:].rearrange("p c t -> p (c t)")
+        quantise(nc, wk_codes[:, :PART], wk_scales[:, :PART], wk_flat[:, : PART * PACK])
         quantise(nc, x_codes[:], x_scales[:], x_grouped[:])
+        quantise(nc, wk_codes[:, PART:], wk_scales[:, PART:], wk_flat[:, PART * PACK :])
         bias_sum = psum_sums.tile([P, K], F32)
         nc.tensor.matmul(out=bias_sum[:], lhsT=ones[:], rhs=bias_rows[:], start=True, stop=True)
         nc.vector.tensor_copy(out=bias[:], in_=bias_sum[:])
-        z_sum = psum_sums.tile([P, K], F32)
-        multiply(z_sum[:], x_codes[:], x_scales[:], wk_codes[:], wk_scales[:])
+        z_sums = []
+        for h in range(K // PART):
+            columns = slice(PART * h, PART * (h + 1))
+            z_half = psum_sums.tile([P, BANK], F32, tag=SIMS_BANKS[1 + h])
+            multiply(z_half[:, :PART], x_codes[:], x_scales[:], wk_codes[:, columns], wk_scales[:, columns])
+            z_sums.append(z_half)
         square_scalar(1, 0)
         square_scalar(1, 1)
         root(1, 1)
-        for g in range(2, PAIRS):
-            square_scalar(g, 0)
-            square_scalar(g, 1)
-        root(2, PAIRS - 1)
+        square_scalar(2, 0)
+        square_scalar(2, 1)
+        square_scalar(3, 0)
+        square_vector(3, 1)
+        root(2, 3)
+        for h in range(K // PART):
+            columns = slice(PART * h, PART * (h + 1))
+            nc.vector.tensor_tensor(out=z[:, columns], in0=z_sums[h][:, :PART], in1=bias[:, columns], op=ALU.add)
         normalise(0)
         transpose_pair(0)
-        nc.vector.tensor_tensor(out=z[:], in0=z_sum[:], in1=bias[:], op=ALU.add)
 
         nc.vector.tensor_scalar(
             out=minus_2z[:], in0=z[:], scalar1=-2.0, scalar2=None, op0=ALU.mult, op1=ALU.min, accum_out=minus_2max[:]
         )
 
-        interleave(0, nc.vector.tensor_copy)
         nc.vector.tensor_scalar_mul(out=minus_max[:], in0=minus_2max[:], scalar1=0.5)
-
         nc.scalar.activation(
             out=e_squared[:], in_=z[:], func=ACT.Exp, bias=minus_2max[:], scale=2.0, accum_out=e_sum_squares[:]
         )
-        nc.scalar.activation(out=e[:], in_=z[:], func=ACT.Exp, bias=minus_max[:], scale=1.0)
+        for u in range(HALVES):
+            columns = slice(K // HALVES * u, K // HALVES * (u + 1))
+            nc.scalar.activation(out=e[:, columns], in_=z[:, columns], func=ACT.Exp, bias=minus_max[:], scale=1.0)
         nc.gpsimd.tensor_tensor(
             out=e_inverse_length[:], in0=e_sum_squares[:], in1=minus_half[:, 0:1], op=ALU.pow
         )
-
         normalise(1)
         transpose_pair(1)
+        interleave(0, nc.vector.tensor_copy)
+
         normalise(2)
         transpose_pair(2)
         normalise(3)
 
-        nc.vector.tensor_scalar(
-            out=kn_rows[:], in0=e[:], scalar1=e_inverse_length[:, 0:1], scalar2=None, op0=ALU.mult
-        )
         kn_planes = psum_words.tile([P, HALVES, P], F32, tag="planes")
-        transpose_words(nc, identity[:], kn_planes, kn_rows[:])
+        for u in range(HALVES):
+            columns = slice(K // HALVES * u, K // HALVES * (u + 1))
+            nc.vector.tensor_scalar(
+                out=kn_rows[:, columns], in0=e[:, columns], scalar1=e_inverse_length[:, 0:1], scalar2=None, op0=ALU.mult
+            )
+            nc.tensor.transpose(kn_planes[:, u, :], kn_rows[:].bitcast(F32)[:, u * P : (u + 1) * P], identity[:])
 
         transpose_pair(3)
         quantise_pair(0)

from contextlib import ExitStack

import concourse.mybir as mybir
from concourse.masks import make_identity

F32 = mybir.dt.float32
BF16 = mybir.dt.bfloat16
U32 = mybir.dt.uint32
U8 = mybir.dt.uint8
FP8X4 = mybir.dt.float8_e4m3fn_x4
ALU = mybir.AluOpType
ACT = mybir.ActivationFunctionType
AXIS_X = mybir.AxisListType.X

P = 128
K = 512
PACK = 4
WORD = 2
HALVES = 2
SLOTS = 1024
BANK = 512
PAIR = 2
PAIRS = SLOTS // (PAIR * P)
TILES = SLOTS // P
WORD_BANKS = 4
NORM_FLOOR = 1e-12
PART = PAIR * P
SIMS_BANKS = ("bias_sum", "z_sum", "sims_a", "sims_b")
RUN = 4

FLOPS = 2 * P * K * K + 2 * P * K * SLOTS


def transpose_words(nc, identity, planes, rows):
    words = rows.bitcast(F32)
    for u in range(HALVES):
        nc.tensor.transpose(planes[:, u, :], words[:, u * P : (u + 1) * P], identity)


def quantise(nc, codes, scales, grouped):
    nc.vector.quantize_mx(out=codes.bitcast(FP8X4), scales=scales, in_=grouped)


def tile_contentaddressablewritehead_pa_s_kernel(tc, controller_output, Wk, bk, memory, out):
    nc = tc.nc
    with ExitStack() as ctx:
        const = ctx.enter_context(tc.tile_pool(name="const", bufs=1))
        keep = ctx.enter_context(tc.tile_pool(name="keep", bufs=1))
        pairs = ctx.enter_context(tc.tile_pool(name="pairs", bufs=PAIRS))
        psum_words = ctx.enter_context(tc.psum_pool(name="psum_words", bufs=WORD_BANKS))
        psum_sums = ctx.enter_context(tc.psum_pool(name="psum_sums", bufs=1))
        ctx.enter_context(tc.manual_schedule())

        memory_tiles = memory.rearrange("(j p) k -> p j k", p=P)
        out_rows = out.flatten_outer_dims()
        memory_pairs = []
        for g in range(PAIRS):
            memory_pair = pairs.tile([P, PAIR, K], BF16)
            memory_pairs.append(memory_pair)
        wk_rows = keep.tile([P, PACK, K], BF16)
        x_rows = keep.tile([P, K], BF16)
        bias_rows = const.tile([P, K], BF16)
        minus_half = const.tile([P, TILES], F32)
        sum_squares = keep.tile([P, TILES], F32)
        floored = keep.tile([P, TILES], F32)
        inverse_length = keep.tile([P, TILES], F32)
        identity = const.tile([P, P], F32)
        ones = const.tile([P, P], BF16)
        table_warmer = const.tile([P, 1], F32)
        mn_codes = keep.tile([P, SLOTS], U32, align_bytes=64)
        mn_scales = keep.tile([P, SLOTS], U8, align_bytes=64)
        rows_of_pair = {}
        planes_of_pair = {}
        grouped_of_pair = {}

        def load_memory(g):
            nc.sync.dma_start(out=memory_pairs[g][:], in_=memory_tiles[:, PAIR * g : PAIR * (g + 1), :])

        def load_wk():
            nc.sync.dma_start(
                out=wk_rows[:].rearrange("p (u e) c -> p u (e c)", u=HALVES),
                in_=Wk.rearrange("(u p e) c -> p u (e c)", u=HALVES, e=WORD),
            )

        def load_x():
            nc.sync.dma_start(out=x_rows[:], in_=controller_output.flatten_outer_dims())

        def square_scalar(g, i):
            squares = pairs.tile([P, K], BF16, tag="squares_s")
            nc.scalar.activation(
                out=squares[:],
                in_=memory_pairs[g][:, i, :],
                func=ACT.Square,
                accum_out=sum_squares[:, PAIR * g + i : PAIR * g + i + 1],
            )

        def square_vector(g, i):
            squares = pairs.tile([P, K], F32, tag="squares_v")
            nc.vector.scalar_tensor_tensor(
                out=squares[:],
                in0=memory_pairs[g][:, i, :],
                scalar=1.0,
                in1=memory_pairs[g][:, i, :],
                op0=ALU.mult,
                op1=ALU.mult,
                accum_out=sum_squares[:, PAIR * g + i : PAIR * g + i + 1],
            )

        def root(first, last):
            tiles = slice(PAIR * first, PAIR * (last + 1))
            nc.gpsimd.tensor_scalar_max(out=floored[:, tiles], in0=sum_squares[:, tiles], scalar1=NORM_FLOOR)
            nc.gpsimd.tensor_tensor(
                out=inverse_length[:, tiles], in0=floored[:, tiles], in1=minus_half[:, tiles], op=ALU.pow
            )

        def normalise(g):
            mn_rows = pairs.tile([P, PAIR, K], BF16)
            for i in range(PAIR):
                nc.vector.tensor_scalar(
                    out=mn_rows[:, i, :],
                    in0=memory_pairs[g][:, i, :],
                    scalar1=inverse_length[:, PAIR * g + i : PAIR * g + i + 1],
                    scalar2=None,
                    op0=ALU.mult,
                )
            rows_of_pair[g] = mn_rows

        def transpose_pair(g):
            mn_planes = psum_words.tile([P, PAIR, HALVES, P], F32, tag="planes")
            for i in range(PAIR):
                transpose_words(nc, identity[:], mn_planes[:, i, :, :], rows_of_pair[g][:, i, :])
            planes_of_pair[g] = mn_planes

        def interleave(g, copy):
            mn_grouped = pairs.tile([P, PAIR * P * PACK], BF16, align_bytes=64)
            copy(
                out=mn_grouped[:].bitcast(F32).rearrange("p (i r u) -> p i r u", i=PAIR, u=HALVES),
                in_=planes_of_pair[g][:].rearrange("p i u r -> p i r u"),
            )
            grouped_of_pair[g] = mn_grouped

        def quantise_pair(g):
            pair_slots = slice(PAIR * P * g, PAIR * P * (g + 1))
            quantise(nc, mn_codes[:, pair_slots], mn_scales[:, pair_slots], grouped_of_pair[g][:])

        wk_grouped = keep.tile([P, K, PACK], BF16, align_bytes=64)
        x_grouped = keep.tile([P, P * PACK], BF16, align_bytes=64)
        wk_codes = keep.tile([P, K], U32, align_bytes=64)
        wk_scales = keep.tile([P, K], U8, align_bytes=64)
        x_codes = keep.tile([P, P], U32, align_bytes=64)
        x_scales = keep.tile([P, P], U8, align_bytes=64)
        bias = const.tile([P, K], F32)
        z = keep.tile([P, K], F32)
        minus_2z = keep.tile([P, K], F32)
        minus_2max = keep.tile([P, 1], F32)
        minus_max = keep.tile([P, 1], F32)
        e_squared = keep.tile([P, K], BF16)
        e_sum_squares = keep.tile([P, 1], F32)
        e = keep.tile([P, K], F32)
        e_inverse_length = keep.tile([P, 1], F32)
        kn_rows = keep.tile([P, K], BF16)
        kn_grouped = keep.tile([P, P * PACK], BF16, align_bytes=64)
        kn_codes = keep.tile([P, P], U32, align_bytes=64)
        kn_scales = keep.tile([P, P], U8, align_bytes=64)
        weights = keep.tile([P, SLOTS], F32)

        def regroup_wk():
            nc.vector.tensor_copy(
                out=wk_grouped[:].rearrange("p (c i) t -> p c t i", i=RUN),
                in_=wk_rows[:].rearrange("p t (c i) -> p c t i", i=RUN),
            )

        def copy_words(copy, grouped, planes):
            copy(
                out=grouped[:].bitcast(F32).rearrange("p (r u) -> p r u", u=HALVES),
                in_=planes[:].rearrange("p u r -> p r u"),
            )

        def multiply(sums, lhs_codes, lhs_scales, rhs_codes, rhs_scales):
            nc.tensor.matmul_mx(
                out=sums,
                lhsT=lhs_codes.bitcast(FP8X4),
                lhsT_scale=lhs_scales,
                rhs=rhs_codes.bitcast(FP8X4),
                rhs_scale=rhs_scales,
                start=True,
                stop=True,
            )

        nc.vector.memset(bias_rows[:], 0.0)
        load_memory(0)
        load_wk()
        load_x()
        nc.sync.dma_start(out=bias_rows[0:1, :], in_=bk.rearrange("(o m) -> o m", o=1))
        for g in range(1, PAIRS):
            load_memory(g)

        nc.vector.memset(minus_half[:], -0.5)
        make_identity(nc, identity[:])
        nc.vector.memset(ones[:], 1.0)
        nc.scalar.activation(out=table_warmer[:], in_=minus_half[:, 0:1], func=ACT.Exp)

        square_scalar(0, 0)
        square_scalar(0, 1)
        root(0, 0)
        regroup_wk()
        x_planes = psum_words.tile([P, HALVES, P], F32, tag="planes")
        transpose_words(nc, identity[:], x_planes, x_rows[:])
        copy_words(nc.vector.tensor_copy, x_grouped, x_planes)
        wk_flat = wk_grouped[:].rearrange("p c t -> p (c t)")
        quantise(nc, wk_codes[:, :PART], wk_scales[:, :PART], wk_flat[:, : PART * PACK])
        quantise(nc, x_codes[:], x_scales[:], x_grouped[:])
        quantise(nc, wk_codes[:, PART:], wk_scales[:, PART:], wk_flat[:, PART * PACK :])
        bias_sum = psum_sums.tile([P, K], F32)
        nc.tensor.matmul(out=bias_sum[:], lhsT=ones[:], rhs=bias_rows[:], start=True, stop=True)
        nc.vector.tensor_copy(out=bias[:], in_=bias_sum[:])
        z_sums = []
        for h in range(K // PART):
            columns = slice(PART * h, PART * (h + 1))
            z_half = psum_sums.tile([P, BANK], F32, tag=SIMS_BANKS[1 + h])
            multiply(z_half[:, :PART], x_codes[:], x_scales[:], wk_codes[:, columns], wk_scales[:, columns])
            z_sums.append(z_half)
        square_scalar(1, 0)
        square_scalar(1, 1)
        root(1, 1)
        square_scalar(2, 0)
        square_scalar(2, 1)
        square_scalar(3, 0)
        square_vector(3, 1)
        root(2, 3)
        for h in range(K // PART):
            columns = slice(PART * h, PART * (h + 1))
            nc.vector.tensor_tensor(out=z[:, columns], in0=z_sums[h][:, :PART], in1=bias[:, columns], op=ALU.add)
        normalise(0)
        transpose_pair(0)

        nc.vector.tensor_scalar(
            out=minus_2z[:], in0=z[:], scalar1=-2.0, scalar2=None, op0=ALU.mult, op1=ALU.min, accum_out=minus_2max[:]
        )

        nc.vector.tensor_scalar_mul(out=minus_max[:], in0=minus_2max[:], scalar1=0.5)
        nc.scalar.activation(
            out=e_squared[:], in_=z[:], func=ACT.Exp, bias=minus_2max[:], scale=2.0, accum_out=e_sum_squares[:]
        )
        for u in range(HALVES):
            columns = slice(K // HALVES * u, K // HALVES * (u + 1))
            nc.scalar.activation(out=e[:, columns], in_=z[:, columns], func=ACT.Exp, bias=minus_max[:], scale=1.0)
        nc.gpsimd.tensor_tensor(
            out=e_inverse_length[:], in0=e_sum_squares[:], in1=minus_half[:, 0:1], op=ALU.pow
        )
        normalise(1)
        transpose_pair(1)
        interleave(0, nc.vector.tensor_copy)

        normalise(2)
        transpose_pair(2)
        normalise(3)

        kn_planes = psum_words.tile([P, HALVES, P], F32, tag="planes")
        for u in range(HALVES):
            columns = slice(K // HALVES * u, K // HALVES * (u + 1))
            nc.vector.tensor_scalar(
                out=kn_rows[:, columns], in0=e[:, columns], scalar1=e_inverse_length[:, 0:1], scalar2=None, op0=ALU.mult
            )
            nc.tensor.transpose(kn_planes[:, u, :], kn_rows[:].bitcast(F32)[:, u * P : (u + 1) * P], identity[:])

        transpose_pair(3)
        quantise_pair(0)
        interleave(1, nc.scalar.copy)
        interleave(2, nc.scalar.copy)
        copy_words(nc.vector.tensor_copy, kn_grouped, kn_planes)
        interleave(3, nc.scalar.copy)
        quantise_pair(1)
        quantise(nc, kn_codes[:], kn_scales[:], kn_grouped[:])
        quantise_pair(2)
        quantise_pair(3)

        part_min = keep.tile([P, PAIRS], F32)
        part_sum = keep.tile([P, PAIRS], F32)
        sims = []
        for g in range(PAIRS):
            part = slice(PART * g, PART * (g + 1))
            sims_part = psum_sums.tile([P, BANK], F32, tag=SIMS_BANKS[g])
            multiply(sims_part[:, :PART], kn_codes[:], kn_scales[:], mn_codes[:, part], mn_scales[:, part])
            sims.append(sims_part)
        for g in range(PAIRS):
            part = slice(PART * g, PART * (g + 1))
            nc.vector.tensor_reduce(out=part_min[:, g : g + 1], in_=sims[g][:, :PART], axis=AXIS_X, op=ALU.min)
            nc.scalar.activation(
                out=weights[:, part],
                in_=sims[g][:, :PART],
                func=ACT.Exp,
                bias=part_min[:, g : g + 1],
                scale=-1.0,
                accum_out=part_sum[:, g : g + 1],
            )
        row_min = keep.tile([P, 1], F32)
        nc.vector.tensor_reduce(out=row_min[:], in_=part_min[:], axis=AXIS_X, op=ALU.min)
        factors = keep.tile([P, PAIRS], F32)
        nc.scalar.activation(out=factors[:], in_=part_min[:], func=ACT.Exp, bias=row_min[:], scale=-1.0)
        scaled_sums = keep.tile([P, PAIRS], F32)
        row_sum = keep.tile([P, 1], F32)
        nc.vector.scalar_tensor_tensor(
            out=scaled_sums[:],
            in0=factors[:],
            scalar=1.0,
            in1=part_sum[:],
            op0=ALU.mult,
            op1=ALU.mult,
            accum_out=row_sum[:],
        )
        inverse_sum = keep.tile([P, 1], F32)
        nc.vector.reciprocal(out=inverse_sum[:], in_=row_sum[:])
        for b in reversed(range(SLOTS // BANK)):
            for g in reversed(range(BANK // PART * b, BANK // PART * (b + 1))):
                part = slice(PART * g, PART * (g + 1))
                nc.vector.tensor_scalar(
                    out=weights[:, part],
                    in0=weights[:, part],
                    scalar1=factors[:, g : g + 1],
                    scalar2=inverse_sum[:, 0:1],
                    op0=ALU.mult,
                    op1=ALU.mult,
                )
            bank_slots = slice(BANK * b, BANK * (b + 1))
            nc.sync.dma_start(out=out_rows[:, bank_slots], in_=weights[:, bank_slots])
